import numpy as np
import ml_dtypes


BF16 = ml_dtypes.bfloat16


def bf(x):
    return np.asarray(x, np.float32).astype(BF16)


def f64(x):
    return np.asarray(x).astype(np.float64)


E2M1 = np.array([0.0, 0.5, 1.0, 1.5, 2.0, 3.0, 4.0, 6.0, -0.0, -0.5, -1.0, -1.5, -2.0, -3.0, -4.0, -6.0])


def pack_weight(w, fmt):
    k, n = w.shape
    w = f64(bf(w)).reshape(k // 32, 32, n)
    amax = np.abs(w).max(1)
    if fmt == "e4m3":
        byte = np.frexp(amax)[1] - 1 + 127 - 7
    else:
        mant, ex = np.frexp(amax / 6.0)
        byte = np.where(mant > 0.5, ex, ex - 1) + 127
    byte = np.clip(np.where(amax > 0, byte, 1), 1, 254)
    scaled = (w * np.exp2(127.0 - byte)[:, None, :]).reshape(k, n).astype(np.float32)
    by_word = np.ascontiguousarray(scaled.reshape(k // 512, 128, 4, n).transpose(0, 1, 3, 2))
    if fmt == "e4m3":
        words = by_word.astype(ml_dtypes.float8_e4m3fn).view(np.uint8)
    else:
        c = by_word.astype(ml_dtypes.float4_e2m1fn).view(np.uint8) & 0xF
        words = c[..., 0::2] | (c[..., 1::2] << 4)
    return np.ascontiguousarray(words), np.ascontiguousarray(byte.astype(np.uint8).reshape(k // 512, 16, n))


def unpack_weight(words, scales, fmt):
    g, p, n, _ = words.shape
    if fmt == "e4m3":
        vals = np.ascontiguousarray(words).view(ml_dtypes.float8_e4m3fn).astype(np.float64)
    else:
        nib = np.empty((g, p, n, 4), np.uint8)
        nib[..., 0::2] = words & 0xF
        nib[..., 1::2] = words >> 4
        vals = E2M1[nib]
    vals = vals * np.repeat(np.exp2(scales.astype(np.float64) - 127.0), 8, axis=1)[..., None]
    return vals.transpose(0, 1, 3, 2).reshape(g * 512, n)

def pack4(w):
    words, scales = pack_weight(w, "e2m1")
    return words.reshape(words.shape[0], 128, -1), scales


def unpack4(words, scales):
    return unpack_weight(words.reshape(words.shape[0], 128, -1, 2), scales, "e2m1")


def kspread(k):
    return np.exp2(np.repeat(np.random.randint(-6, 7, k // 32), 32).astype(np.float64))


B, S, D, H = 1, 1536, 2048, 16
HD = D // H
HALF = HD // 2
ROPE_BASE = 10000.0


def apply_rope(x, cos, sin):
    x1, x2 = np.split(x, 2, axis=-1)
    c = cos[None, None]
    s = sin[None, None]
    return np.concatenate([x1 * c - x2 * s, x1 * s + x2 * c], axis=-1)


def setup_inputs():
    s = kspread(D)
    inv_freq = 1.0 / (ROPE_BASE ** (f64(np.arange(HALF)) / HALF))
    pos = f64(np.random.randint(0, S) + np.arange(S))
    ang = pos[:, None] * inv_freq[None, :]
    x = np.random.standard_normal((B, S, D)) * s
    x_words, x_scales = pack4(x.reshape(B * S, D).T)
    words, scales = pack4(np.random.standard_normal((D, 3 * D)) / np.sqrt(D) / s[:, None])
    return {"x_words": x_words,
            "x_scales": x_scales,
            "w_qkv_words": words,
            "w_qkv_scales": scales,
            "b_qkv": bf(np.random.standard_normal(3 * D) * 0.5),
            "rope_cos": bf(np.cos(ang)),
            "rope_sin": bf(np.sin(ang))}


def reference(x_words, x_scales, w_qkv_words, w_qkv_scales, b_qkv, rope_cos, rope_sin):
    cos, sin = f64(rope_cos), f64(rope_sin)
    x = unpack4(x_words, x_scales).T.reshape(B, S, D)
    qkv = (x @ unpack4(w_qkv_words, w_qkv_scales)) + f64(b_qkv)
    qkv = qkv.reshape(B, S, 3, H, HD)
    qkv = np.transpose(qkv, (2, 0, 3, 1, 4))
    q, k, v = qkv[0], qkv[1], qkv[2]
    return apply_rope(q, cos, sin), apply_rope(k, cos, sin), np.ascontiguousarray(v)

@@ -1,0 +1,261 @@
+from contextlib import ExitStack
+
+import concourse.mybir as mybir
+from concourse.masks import make_identity
+
+F32 = mybir.dt.float32
+BF16 = mybir.dt.bfloat16
+U8 = mybir.dt.uint8
+I32 = mybir.dt.int32
+FP4X4 = mybir.dt.float4_e2m1fn_x4
+ADD = mybir.AluOpType.add
+MULT = mybir.AluOpType.mult
+
+S, D, HD = 1536, 2048, 128
+HALF = HD // 2
+FLOPS = 2 * S * D * 3 * D
+
+P = 128
+PASSES = D // 512
+BLOCK = 512
+WINDOWS = 4
+PAIRS = S // (2 * P)
+X_PLANE_SPLITS = ((0, 4), (4, 12))
+X_CODE_SPLITS = ((0, 2), (2, 4), (4, 12))
+V_HELD_BACK = 3
+POOL_SINE_GROUPS = 21
+POOL_SINE_SKIP = 10
+
+
+def tile_multiheadattentionusingsdp_pa_kernel(
+    tc, x_words, x_scales, w_qkv_words, w_qkv_scales, b_qkv, rope_cos, rope_sin, out_0, out_1, out_2
+):
+    nc = tc.nc
+    outs = (out_0, out_1, out_2)
+    with ExitStack() as ctx:
+        keep = ctx.enter_context(tc.tile_pool(name="keep", bufs=1))
+        stream = ctx.enter_context(tc.tile_pool(name="stream", bufs=2))
+        work = ctx.enter_context(tc.tile_pool(name="work", bufs=4))
+        acc_pool = ctx.enter_context(tc.psum_pool(name="acc", bufs=5))
+        tab_pool = ctx.enter_context(tc.psum_pool(name="tab", bufs=1))
+        ctx.enter_context(tc.manual_schedule())
+
+        x_codes = [
+            keep.tile([P, PASSES, 256 * (t1 - t0)], U8, name="x_codes%d" % i, align_bytes=64)
+            for i, (t0, t1) in enumerate(X_CODE_SPLITS)
+        ]
+        x_planes = [
+            keep.tile([P, PASSES, P * (t1 - t0)], U8, name="x_planes%d" % i, align_bytes=64)
+            for i, (t0, t1) in enumerate(X_PLANE_SPLITS)
+        ]
+        w_planes = [keep.tile([P, PASSES, 2 * BLOCK], U8, name="w_planes%d" % c, align_bytes=64) for c in range(6)]
+        bias = [keep.tile([P, 2 * BLOCK], BF16, name="bias%d" % c) for c in range(6)]
+        tabs = keep.tile([P, 12, 2 * HD], BF16, name="tabs")
+        ident = keep.tile([P, P], BF16, name="ident")
+
+        nc.vector.memset(x_planes[0][:].bitcast(I32), 0)
+        for c in (0, 4, 1, 2, 5, 3):
+            nc.vector.memset(w_planes[c][:].bitcast(I32), 0)
+        nc.vector.memset(x_planes[1][:].bitcast(I32), 0)
+
+        make_identity(nc, ident[:])
+        for k, table in enumerate((rope_cos, rope_cos, rope_sin, rope_sin)):
+            nc.gpsimd.dma_start(
+                out=tabs[:, :, HALF * k : HALF * (k + 1)], in_=table.rearrange("(t p) d -> p t d", p=P)
+            )
+        nc.scalar.mul(out=tabs[:, :, HD : HD + HALF], in_=tabs[:, :, HD : HD + HALF], mul=-1.0)
+
+        def load_planes(planes, scales, c0, c1):
+            for q in range(4):
+                nc.sync.dma_start(
+                    out=planes[32 * q : 32 * q + 4, :, :].bitcast(I32),
+                    in_=scales[:, 4 * q : 4 * q + 4, c0:c1].rearrange("g r n -> r g n").bitcast(I32),
+                )
+
+        def load_codes(codes, words, c0, c1):
+            nc.sync.dma_start(
+                out=codes[:].bitcast(I32),
+                in_=words[:, :, 2 * c0 : 2 * c1].rearrange("g p n -> p g n").bitcast(I32),
+            )
+
+        def load_x_planes(i):
+            t0, t1 = X_PLANE_SPLITS[i]
+            load_planes(x_planes[i], x_scales, P * t0, P * t1)
+
+        def load_x_codes(i):
+            t0, t1 = X_CODE_SPLITS[i]
+            load_codes(x_codes[i], x_words, P * t0, P * t1)
+
+        def load_chunk_planes(c):
+            load_planes(w_planes[c], w_qkv_scales, 2 * BLOCK * c, 2 * BLOCK * (c + 1))
+
+        def load_bias(c):
+            nc.sync.dma_start(out=bias[c][:], in_=b_qkv[2 * BLOCK * c : 2 * BLOCK * (c + 1)].partition_broadcast(P))
+
+        w_codes = {}
+
+        def load_block(j, tag):
+            w_codes[j] = stream.tile([P, PASSES, 2 * BLOCK], U8, name=tag, align_bytes=64)
+            load_codes(w_codes[j], w_qkv_words, BLOCK * j, BLOCK * (j + 1))
+
+        def load_window(w):
+            load_chunk_planes(w)
+            if w == 0:
+                load_x_codes(0)
+            load_block(2 * w, "w_first")
+            load_bias(w)
+            load_block(2 * w + 1, "w_second")
+            if w % 2 == 0:
+                load_chunk_planes(4 + w // 2)
+            load_block(8 + w, "w_value")
+            if w % 2 == 0:
+                load_bias(4 + w // 2)
+
+        load_x_planes(0)
+        load_window(0)
+        load_x_codes(1)
+        load_x_planes(1)
+        load_x_codes(2)
+        load_window(1)
+
+        tables = []
+        pending = []
+        head = [0]
+
+        def make_tables():
+            for q in range(3):
+                t = tab_pool.tile([P, 8 * HD], BF16, name="tab%d" % q)
+                for k in range(2):
+                    nc.tensor.matmul(
+                        out=t[:, 4 * HD * k : 4 * HD * (k + 1)],
+                        lhsT=ident[:],
+                        rhs=tabs[:, 4 * q + 2 * k : 4 * q + 2 * k + 2, :].rearrange("p t n -> p (t n)"),
+                        start=True,
+                        stop=True,
+                    )
+                tables.append(t)
+
+        def window_of(tiles_of, splits, t, g, width):
+            i = [k for k, (t0, t1) in enumerate(splits) if t0 <= t < t1][0]
+            c0 = width * (t - splits[i][0])
+            return tiles_of[i][:, g, c0 : c0 + width]
+
+        def project(t, j):
+            acc = acc_pool.tile([P, BLOCK], F32, name="acc")
+            o = BLOCK * (j % 2)
+            for g in range(PASSES):
+                nc.tensor.matmul_mx(
+                    out=acc[:],
+                    lhsT=window_of(x_codes, X_CODE_SPLITS, t, g, 256).bitcast(FP4X4),
+                    lhsT_scale=window_of(x_planes, X_PLANE_SPLITS, t, g, P),
+                    rhs=w_codes[j][:, g, :].bitcast(FP4X4),
+                    rhs_scale=w_planes[j // 2][:, g, o : o + BLOCK],
+                    start=(g == 0),
+                    stop=(g == PASSES - 1),
+                )
+            return acc
+
+        def add_bias(dst, acc, j):
+            o = BLOCK * (j % 2)
+            nc.vector.tensor_tensor(out=dst, in0=acc[:], in1=bias[j // 2][:, o : o + BLOCK], op=ADD)
+
+        def store(which, h0, nh, t, src):
+            nc.scalar.dma_start(
+                out=outs[which][0, h0 : h0 + nh, P * t : P * (t + 1), :].rearrange("h s d -> s h d"),
+                in_=src.rearrange("p (h d) -> p h d", d=HD),
+            )
+
+        def cosine_product(grp, tt):
+            t = 2 * grp["pair"] + tt
+            cos = tables[t // 4][:, 2 * HD * (t % 4) : 2 * HD * (t % 4) + HD]
+            nc.vector.tensor_tensor(
+                out=grp["m"][:, tt, :].rearrange("p (h d) -> p h d", d=HD),
+                in0=grp["u"][:, tt, :].rearrange("p (h d) -> p h d", d=HD),
+                in1=cos.unsqueeze(1).to_broadcast([P, 8, HD]),
+                op=MULT,
+            )
+
+        def sine_product(grp, half, on_pool):
+            pair = grp["pair"]
+            u4 = grp["u"][:].rearrange("p t (h d) -> p t h d", d=HD)
+            w4 = grp["w"][:].rearrange("p t (h d) -> p t h d", d=HD)
+            dst = w4[:, :, :, HALF * half : HALF * (half + 1)]
+            src = u4[:, :, :, HALF * (1 - half) : HALF * (2 - half)]
+            c0 = HD + HALF * half
+            if on_pool:
+                sin = tabs[:, 2 * pair : 2 * pair + 2, c0 : c0 + HALF]
+            else:
+                k = 2 * (pair % 2)
+                sin = tables[pair // 2][:].rearrange("p (t n) -> p t n", t=4)[:, k : k + 2, c0 : c0 + HALF]
+            engine = nc.gpsimd if on_pool else nc.vector
+            engine.tensor_tensor(out=dst, in0=src, in1=sin.unsqueeze(2).to_broadcast([P, 2, 8, HALF]), op=MULT)
+
+        def finish_group(grp):
+            mv = grp["m"][:].rearrange("p t n -> p (t n)")
+            wv = grp["w"][:].rearrange("p t n -> p (t n)")
+            engine = nc.vector if grp["last"] else nc.gpsimd
+            engine.tensor_tensor(out=mv, in0=mv, in1=wv, op=ADD)
+            w = grp["window"]
+            for tt in range(2):
+                store(w // 2, 8 * (w % 2), 8, 2 * grp["pair"] + tt, grp["m"][:, tt, :])
+
+        def pop_pending(now):
+            if head[0] < len(pending) and pending[head[0]][0] < now:
+                grp, what, k = pending[head[0]][1]
+                head[0] += 1
+                if what == "cos":
+                    cosine_product(grp, k)
+                else:
+                    sine_product(grp, k, False)
+                grp["left"] -= 1
+                if grp["left"] == 0:
+                    finish_group(grp)
+
+        step = 0
+        n_groups = 0
+        for w in range(WINDOWS):
+            woven = PAIRS - V_HELD_BACK if w == WINDOWS - 1 else PAIRS
+            order = [(kind, pair) for pair in range(woven) for kind in ("r", "v")]
+            order += [("r", pair) for pair in range(woven, PAIRS)] + [("v", pair) for pair in range(woven, PAIRS)]
+            for kind, pair in order:
+                if kind == "r":
+                    grp = {
+                        "pair": pair,
+                        "window": w,
+                        "last": n_groups == WINDOWS * PAIRS - 1,
+                        "u": work.tile([P, 2, 2 * BLOCK], F32, name="u", bufs=5),
+                        "m": work.tile([P, 2, 2 * BLOCK], F32, name="m", bufs=7),
+                        "w": work.tile([P, 2, 2 * BLOCK], F32, name="w", bufs=4),
+                        "left": 4,
+                    }
+                    for j in (2 * w, 2 * w + 1):
+                        for tt in range(2):
+                            acc = project(2 * pair + tt, j)
+                            if step == 3:
+                                make_tables()
+                            o = BLOCK * (j % 2)
+                            add_bias(grp["u"][:, tt, o : o + BLOCK], acc, j)
+                            pop_pending(step)
+                            step += 1
+                    on_pool = n_groups < POOL_SINE_GROUPS and n_groups % POOL_SINE_SKIP != POOL_SINE_SKIP - 1
+                    n_groups += 1
+                    pending.append((step - 1, (grp, "cos", 0)))
+                    pending.append((step - 1, (grp, "cos", 1)))
+                    pending.append((step - 1, (grp, "sin", 0)))
+                    if on_pool:
+                        grp["left"] -= 1
+                        sine_product(grp, 1, True)
+                    else:
+                        pending.append((step - 1, (grp, "sin", 1)))
+                else:
+                    v = work.tile([P, 2, BLOCK], F32, name="v", bufs=5)
+                    for tt in range(2):
+                        acc = project(2 * pair + tt, 8 + w)
+                        add_bias(v[:, tt, :], acc, 8 + w)
+                        store(2, 4 * w, 4, 2 * pair + tt, v[:, tt, :])
+                        pop_pending(step)
+                        step += 1
+            if w + 2 < WINDOWS:
+                load_window(w + 2)
+        while head[0] < len(pending):
+            pop_pending(step)

@@ -9,22 +9,26 @@ U8 = mybir.dt.uint8
 I32 = mybir.dt.int32
 FP4X4 = mybir.dt.float4_e2m1fn_x4
 ADD = mybir.AluOpType.add
+SUB = mybir.AluOpType.subtract
 MULT = mybir.AluOpType.mult
+COPY = mybir.ActivationFunctionType.Copy
 
 S, D, HD = 1536, 2048, 128
 HALF = HD // 2
+HEADS = 16
 FLOPS = 2 * S * D * 3 * D
 
 P = 128
 PASSES = D // 512
 BLOCK = 512
-WINDOWS = 4
-PAIRS = S // (2 * P)
+TILES = S // P
+UNIT = HEADS * HD
 X_PLANE_SPLITS = ((0, 4), (4, 12))
 X_CODE_SPLITS = ((0, 2), (2, 4), (4, 12))
-V_HELD_BACK = 3
-POOL_SINE_GROUPS = 21
-POOL_SINE_SKIP = 10
+V_HELD_BACK = 8
+STORE_LAG = 10
+VECTOR_COMBINES = 1
+VECTOR_COMBINE_LAG = 5
 
 
 def tile_multiheadattentionusingsdp_pa_kernel(
@@ -34,9 +38,8 @@ def tile_multiheadattentionusingsdp_pa_kernel(
     outs = (out_0, out_1, out_2)
     with ExitStack() as ctx:
         keep = ctx.enter_context(tc.tile_pool(name="keep", bufs=1))
-        stream = ctx.enter_context(tc.tile_pool(name="stream", bufs=2))
-        work = ctx.enter_context(tc.tile_pool(name="work", bufs=4))
-        acc_pool = ctx.enter_context(tc.psum_pool(name="acc", bufs=5))
+        work = ctx.enter_context(tc.tile_pool(name="work", bufs=3))
+        acc_pool = ctx.enter_context(tc.psum_pool(name="acc", bufs=6))
         tab_pool = ctx.enter_context(tc.psum_pool(name="tab", bufs=1))
         ctx.enter_context(tc.manual_schedule())
 
@@ -49,21 +52,27 @@ def tile_multiheadattentionusingsdp_pa_kernel(
             for i, (t0, t1) in enumerate(X_PLANE_SPLITS)
         ]
         w_planes = [keep.tile([P, PASSES, 2 * BLOCK], U8, name="w_planes%d" % c, align_bytes=64) for c in range(6)]
+        w_codes = [keep.tile([P, PASSES, 2 * BLOCK], U8, name="w_codes%d" % j, align_bytes=64) for j in range(12)]
         bias = [keep.tile([P, 2 * BLOCK], BF16, name="bias%d" % c) for c in range(6)]
-        tabs = keep.tile([P, 12, 2 * HD], BF16, name="tabs")
+        cos2 = keep.tile([P, TILES, HD], BF16, name="cos2")
+        sin_b = keep.tile([P, TILES, HALF], BF16, name="sin_b")
+        sin_f = keep.tile([P, TILES, HALF], F32, name="sin_f")
         ident = keep.tile([P, P], BF16, name="ident")
 
         nc.vector.memset(x_planes[0][:].bitcast(I32), 0)
-        for c in (0, 4, 1, 2, 5, 3):
+        for c in (0, 1, 4):
             nc.vector.memset(w_planes[c][:].bitcast(I32), 0)
         nc.vector.memset(x_planes[1][:].bitcast(I32), 0)
+        for c in (2, 3, 5):
+            nc.vector.memset(w_planes[c][:].bitcast(I32), 0)
 
         make_identity(nc, ident[:])
-        for k, table in enumerate((rope_cos, rope_cos, rope_sin, rope_sin)):
+        for k in range(2):
             nc.gpsimd.dma_start(
-                out=tabs[:, :, HALF * k : HALF * (k + 1)], in_=table.rearrange("(t p) d -> p t d", p=P)
+                out=cos2[:, :, HALF * k : HALF * (k + 1)], in_=rope_cos.rearrange("(t p) d -> p t d", p=P)
             )
-        nc.scalar.mul(out=tabs[:, :, HD : HD + HALF], in_=tabs[:, :, HD : HD + HALF], mul=-1.0)
+        nc.gpsimd.dma_start(out=sin_b[:], in_=rope_sin.rearrange("(t p) d -> p t d", p=P))
+        nc.scalar.copy(out=sin_f[:], in_=sin_b[:])
 
         def load_planes(planes, scales, c0, c1):
             for q in range(4):
@@ -92,44 +101,38 @@ def tile_multiheadattentionusingsdp_pa_kernel(
         def load_bias(c):
             nc.sync.dma_start(out=bias[c][:], in_=b_qkv[2 * BLOCK * c : 2 * BLOCK * (c + 1)].partition_broadcast(P))
 
-        w_codes = {}
-
-        def load_block(j, tag):
-            w_codes[j] = stream.tile([P, PASSES, 2 * BLOCK], U8, name=tag, align_bytes=64)
+        def load_block(j):
             load_codes(w_codes[j], w_qkv_words, BLOCK * j, BLOCK * (j + 1))
 
-        def load_window(w):
-            load_chunk_planes(w)
-            if w == 0:
-                load_x_codes(0)
-            load_block(2 * w, "w_first")
-            load_bias(w)
-            load_block(2 * w + 1, "w_second")
-            if w % 2 == 0:
-                load_chunk_planes(4 + w // 2)
-            load_block(8 + w, "w_value")
-            if w % 2 == 0:
-                load_bias(4 + w // 2)
+        def load_chunk(c):
+            load_chunk_planes(c)
+            load_block(2 * c)
+            load_bias(c)
+            load_block(2 * c + 1)
 
+        load_x_codes(0)
+        load_block(0)
         load_x_planes(0)
-        load_window(0)
+        load_chunk_planes(0)
+        load_bias(0)
+        load_block(1)
+        load_chunk(1)
         load_x_codes(1)
+        load_chunk(4)
         load_x_planes(1)
         load_x_codes(2)
-        load_window(1)
 
         tables = []
-        pending = []
-        head = [0]
 
         def make_tables():
-            for q in range(3):
-                t = tab_pool.tile([P, 8 * HD], BF16, name="tab%d" % q)
-                for k in range(2):
+            for q, width in enumerate((8, 4)):
+                t = tab_pool.tile([P, width * HD], BF16, name="tab%d" % q)
+                for k in range(width // 4):
+                    t0 = 8 * q + 4 * k
                     nc.tensor.matmul(
                         out=t[:, 4 * HD * k : 4 * HD * (k + 1)],
                         lhsT=ident[:],
-                        rhs=tabs[:, 4 * q + 2 * k : 4 * q + 2 * k + 2, :].rearrange("p t n -> p (t n)"),
+                        rhs=cos2[:, t0 : t0 + 4, :].rearrange("p t n -> p (t n)"),
                         start=True,
                         stop=True,
                     )
@@ -160,102 +163,125 @@ def tile_multiheadattentionusingsdp_pa_kernel(
             nc.vector.tensor_tensor(out=dst, in0=acc[:], in1=bias[j // 2][:, o : o + BLOCK], op=ADD)
 
         def store(which, h0, nh, t, src):
-            nc.scalar.dma_start(
+            nc.sync.dma_start(
                 out=outs[which][0, h0 : h0 + nh, P * t : P * (t + 1), :].rearrange("h s d -> s h d"),
                 in_=src.rearrange("p (h d) -> p h d", d=HD),
             )
 
-        def cosine_product(grp, tt):
-            t = 2 * grp["pair"] + tt
-            cos = tables[t // 4][:, 2 * HD * (t % 4) : 2 * HD * (t % 4) + HD]
+        def cosine_product(unit, part):
+            t = unit["t"]
+            cos = tables[t // 8][:, HD * (t % 8) : HD * (t % 8) + HD]
+            c0 = part * (UNIT // 2)
             nc.vector.tensor_tensor(
-                out=grp["m"][:, tt, :].rearrange("p (h d) -> p h d", d=HD),
-                in0=grp["u"][:, tt, :].rearrange("p (h d) -> p h d", d=HD),
-                in1=cos.unsqueeze(1).to_broadcast([P, 8, HD]),
+                out=unit["m"][:, c0 : c0 + UNIT // 2].rearrange("p (h d) -> p h d", d=HD),
+                in0=unit["u"][:, c0 : c0 + UNIT // 2].rearrange("p (h d) -> p h d", d=HD),
+                in1=cos.unsqueeze(1).to_broadcast([P, HEADS // 2, HD]),
                 op=MULT,
             )
 
-        def sine_product(grp, half, on_pool):
-            pair = grp["pair"]
-            u4 = grp["u"][:].rearrange("p t (h d) -> p t h d", d=HD)
-            w4 = grp["w"][:].rearrange("p t (h d) -> p t h d", d=HD)
-            dst = w4[:, :, :, HALF * half : HALF * (half + 1)]
-            src = u4[:, :, :, HALF * (1 - half) : HALF * (2 - half)]
-            c0 = HD + HALF * half
-            if on_pool:
-                sin = tabs[:, 2 * pair : 2 * pair + 2, c0 : c0 + HALF]
-            else:
-                k = 2 * (pair % 2)
-                sin = tables[pair // 2][:].rearrange("p (t n) -> p t n", t=4)[:, k : k + 2, c0 : c0 + HALF]
-            engine = nc.gpsimd if on_pool else nc.vector
-            engine.tensor_tensor(out=dst, in0=src, in1=sin.unsqueeze(2).to_broadcast([P, 2, 8, HALF]), op=MULT)
+        def sine_products(unit):
+            t = unit["t"]
+            u4 = unit["u"][:].rearrange("p (h f d) -> p h f d", f=2, d=HALF)
+            for d in range(HALF):
+                nc.scalar.activation(
+                    out=unit["w"][:, d, :].rearrange("p (h f) -> p h f", f=2),
+                    in_=u4[:, :, :, d],
+                    func=COPY,
+                    scale=sin_f[:, t, d : d + 1],
+                )
 
-        def finish_group(grp):
-            mv = grp["m"][:].rearrange("p t n -> p (t n)")
-            wv = grp["w"][:].rearrange("p t n -> p (t n)")
-            engine = nc.vector if grp["last"] else nc.gpsimd
-            engine.tensor_tensor(out=mv, in0=mv, in1=wv, op=ADD)
-            w = grp["window"]
-            for tt in range(2):
-                store(w // 2, 8 * (w % 2), 8, 2 * grp["pair"] + tt, grp["m"][:, tt, :])
+        def combine(unit, engine, half):
+            m3 = unit["m"][:].rearrange("p (h d) -> p h d", d=HD)
+            wv = unit["w"][:].rearrange("p d (h f) -> p f h d", f=2)
+            c0 = HALF * half
+            engine.tensor_tensor(
+                out=m3[:, :, c0 : c0 + HALF], in0=m3[:, :, c0 : c0 + HALF], in1=wv[:, 1 - half], op=(ADD if half else SUB)
+            )
 
-        def pop_pending(now):
-            if head[0] < len(pending) and pending[head[0]][0] < now:
-                grp, what, k = pending[head[0]][1]
-                head[0] += 1
-                if what == "cos":
-                    cosine_product(grp, k)
-                else:
-                    sine_product(grp, k, False)
-                grp["left"] -= 1
-                if grp["left"] == 0:
-                    finish_group(grp)
+        def store_unit(unit):
+            store(unit["w_id"], 0, HEADS, unit["t"], unit["m"][:])
 
-        step = 0
-        n_groups = 0
-        for w in range(WINDOWS):
-            woven = PAIRS - V_HELD_BACK if w == WINDOWS - 1 else PAIRS
-            order = [(kind, pair) for pair in range(woven) for kind in ("r", "v")]
-            order += [("r", pair) for pair in range(woven, PAIRS)] + [("v", pair) for pair in range(woven, PAIRS)]
-            for kind, pair in order:
-                if kind == "r":
-                    grp = {
-                        "pair": pair,
-                        "window": w,
-                        "last": n_groups == WINDOWS * PAIRS - 1,
-                        "u": work.tile([P, 2, 2 * BLOCK], F32, name="u", bufs=5),
-                        "m": work.tile([P, 2, 2 * BLOCK], F32, name="m", bufs=7),
-                        "w": work.tile([P, 2, 2 * BLOCK], F32, name="w", bufs=4),
+        rope_units = [(t, w) for w in range(2) for t in range(TILES)]
+        value_jobs = [(t, 8 + 2 * w + k) for w in range(2) for t in range(TILES) for k in range(2)]
+        woven = len(value_jobs) - V_HELD_BACK
+        jobs = [(t, j) for j in range(4) for t in (0, 1)]
+        drawn = 0
+        for i, (t, w) in enumerate(rope_units):
+            if i >= 2:
+                jobs += [(t, 4 * w + k) for k in range(4)]
+            if i >= 1:
+                quota = (woven * (i + 1)) // len(rope_units)
+                jobs += value_jobs[drawn:quota]
+                drawn = quota
+        jobs += value_jobs[drawn:]
+
+        late_loads = {14: 2, 26: 3, 38: 5}
+        units = {}
+        values = {}
+        pending = []
+        deferred = []
+        n_done = 0
+
+        def run_deferred(now):
+            ready = sorted([e for e in deferred if e[0] <= now], key=lambda e: e[0])
+            for e in ready:
+                deferred.remove(e)
+                e[1]()
+
+        def vector_tail(unit, half):
+            combine(unit, nc.vector, half)
+            if half == 1:
+                store_unit(unit)
+
+        for step, (t, j) in enumerate(jobs):
+            acc = project(t, j)
+            if step == 3:
+                make_tables()
+            done = False
+            if j < 8:
+                w = j // 4
+                if (t, w) not in units:
+                    units[(t, w)] = {
+                        "t": t,
+                        "w_id": w,
+                        "u": work.tile([P, UNIT], F32, name="u"),
+                        "m": work.tile([P, UNIT], F32, name="m"),
+                        "w": work.tile([P, HALF, 2 * HEADS], F32, name="w"),
                         "left": 4,
                     }
-                    for j in (2 * w, 2 * w + 1):
-                        for tt in range(2):
-                            acc = project(2 * pair + tt, j)
-                            if step == 3:
-                                make_tables()
-                            o = BLOCK * (j % 2)
-                            add_bias(grp["u"][:, tt, o : o + BLOCK], acc, j)
-                            pop_pending(step)
-                            step += 1
-                    on_pool = n_groups < POOL_SINE_GROUPS and n_groups % POOL_SINE_SKIP != POOL_SINE_SKIP - 1
-                    n_groups += 1
-                    pending.append((step - 1, (grp, "cos", 0)))
-                    pending.append((step - 1, (grp, "cos", 1)))
-                    pending.append((step - 1, (grp, "sin", 0)))
-                    if on_pool:
-                        grp["left"] -= 1
-                        sine_product(grp, 1, True)
-                    else:
-                        pending.append((step - 1, (grp, "sin", 1)))
-                else:
-                    v = work.tile([P, 2, BLOCK], F32, name="v", bufs=5)
-                    for tt in range(2):
-                        acc = project(2 * pair + tt, 8 + w)
-                        add_bias(v[:, tt, :], acc, 8 + w)
-                        store(2, 4 * w, 4, 2 * pair + tt, v[:, tt, :])
-                        pop_pending(step)
-                        step += 1
-            if w + 2 < WINDOWS:
-                load_window(w + 2)
-        while head[0] < len(pending):
-            pop_pending(step)
+                unit = units[(t, w)]
+                o = BLOCK * (j % 4)
+                add_bias(unit["u"][:, o : o + BLOCK], acc, j)
+                unit["left"] -= 1
+                done = unit["left"] == 0
+            else:
+                w = (j - 8) // 2
+                if (t, w) not in values:
+                    values[(t, w)] = work.tile([P, 2 * BLOCK], F32, name="v", bufs=5)
+                v = values[(t, w)]
+                o = BLOCK * (j % 2)
+                add_bias(v[:, o : o + BLOCK], acc, j)
+                if step >= len(jobs) - 2:
+                    store(2, 4 * (j - 8), 4, t, v[:, o : o + BLOCK])
+                elif j % 2 == 1:
+                    store(2, 8 * w, 8, t, v[:])
+            if pending:
+                pu, part = pending.pop(0)
+                cosine_product(pu, part)
+                if part == 1 and not pu["on_vector"]:
+                    combine(pu, nc.gpsimd, 0)
+                    combine(pu, nc.gpsimd, 1)
+                    deferred.append((step + STORE_LAG, lambda u=pu: store_unit(u)))
+            run_deferred(step)
+            if done:
+                n_done += 1
+                unit["on_vector"] = n_done > len(rope_units) - VECTOR_COMBINES
+                sine_products(unit)
+                pending.append((unit, 0))
+                pending.append((unit, 1))
+                if unit["on_vector"]:
+                    deferred.append((step + VECTOR_COMBINE_LAG, lambda u=unit: vector_tail(u, 0)))
+                    deferred.append((step + VECTOR_COMBINE_LAG + 1, lambda u=unit: vector_tail(u, 1)))
+            if step in late_loads:
+                load_chunk(late_loads[step])
+        run_deferred(len(jobs) + 100)

@@ -39,7 +39,7 @@ def tile_multiheadattentionusingsdp_pa_kernel(
     with ExitStack() as ctx:
         keep = ctx.enter_context(tc.tile_pool(name="keep", bufs=1))
         work = ctx.enter_context(tc.tile_pool(name="work", bufs=3))
-        acc_pool = ctx.enter_context(tc.psum_pool(name="acc", bufs=6))
+        acc_pool = ctx.enter_context(tc.psum_pool(name="acc", bufs=7))
         tab_pool = ctx.enter_context(tc.psum_pool(name="tab", bufs=1))
         ctx.enter_context(tc.manual_schedule())
 
@@ -54,11 +54,14 @@ def tile_multiheadattentionusingsdp_pa_kernel(
         w_planes = [keep.tile([P, PASSES, 2 * BLOCK], U8, name="w_planes%d" % c, align_bytes=64) for c in range(6)]
         w_codes = [keep.tile([P, PASSES, 2 * BLOCK], U8, name="w_codes%d" % j, align_bytes=64) for j in range(12)]
         bias = [keep.tile([P, 2 * BLOCK], BF16, name="bias%d" % c) for c in range(6)]
-        cos2 = keep.tile([P, TILES, HD], BF16, name="cos2")
+        cos_b = keep.tile([P, TILES, HALF], BF16, name="cos_b")
+        b_rows = keep.tile([P, 3 * BLOCK], BF16, name="b_rows")
         sin_b = keep.tile([P, TILES, HALF], BF16, name="sin_b")
         sin_f = keep.tile([P, TILES, HALF], F32, name="sin_f")
         ident = keep.tile([P, P], BF16, name="ident")
 
+        nc.vector.memset(b_rows[:], 0.0)
+        nc.scalar.dma_start(out=b_rows[0:4, :], in_=b_qkv.rearrange("(k n) -> k n", k=4))
         nc.vector.memset(x_planes[0][:].bitcast(I32), 0)
         for c in (0, 1, 4):
             nc.vector.memset(w_planes[c][:].bitcast(I32), 0)
@@ -67,12 +70,8 @@ def tile_multiheadattentionusingsdp_pa_kernel(
             nc.vector.memset(w_planes[c][:].bitcast(I32), 0)
 
         make_identity(nc, ident[:])
-        for k in range(2):
-            nc.gpsimd.dma_start(
-                out=cos2[:, :, HALF * k : HALF * (k + 1)], in_=rope_cos.rearrange("(t p) d -> p t d", p=P)
-            )
+        nc.gpsimd.dma_start(out=cos_b[:], in_=rope_cos.rearrange("(t p) d -> p t d", p=P))
         nc.gpsimd.dma_start(out=sin_b[:], in_=rope_sin.rearrange("(t p) d -> p t d", p=P))
-        nc.scalar.copy(out=sin_f[:], in_=sin_b[:])
 
         def load_planes(planes, scales, c0, c1):
             for q in range(4):
@@ -98,8 +97,18 @@ def tile_multiheadattentionusingsdp_pa_kernel(
         def load_chunk_planes(c):
             load_planes(w_planes[c], w_qkv_scales, 2 * BLOCK * c, 2 * BLOCK * (c + 1))
 
-        def load_bias(c):
-            nc.sync.dma_start(out=bias[c][:], in_=b_qkv[2 * BLOCK * c : 2 * BLOCK * (c + 1)].partition_broadcast(P))
+        def spread_bias(c):
+            spread = acc_pool.tile([P, 2 * BLOCK], BF16, name="acc")
+            for half in range(2):
+                n = 2 * c + half
+                nc.tensor.matmul(
+                    out=spread[:, BLOCK * half : BLOCK * (half + 1)],
+                    lhsT=ident[:, n // 3 : n // 3 + 1].to_broadcast([P, P]),
+                    rhs=b_rows[:, BLOCK * (n % 3) : BLOCK * (n % 3 + 1)],
+                    start=True,
+                    stop=True,
+                )
+            nc.scalar.copy(out=bias[c][:], in_=spread[:])
 
         def load_block(j):
             load_codes(w_codes[j], w_qkv_words, BLOCK * j, BLOCK * (j + 1))
@@ -107,14 +116,12 @@ def tile_multiheadattentionusingsdp_pa_kernel(
         def load_chunk(c):
             load_chunk_planes(c)
             load_block(2 * c)
-            load_bias(c)
             load_block(2 * c + 1)
 
         load_x_codes(0)
         load_block(0)
         load_x_planes(0)
         load_chunk_planes(0)
-        load_bias(0)
         load_block(1)
         load_chunk(1)
         load_x_codes(1)
@@ -122,21 +129,25 @@ def tile_multiheadattentionusingsdp_pa_kernel(
         load_x_planes(1)
         load_x_codes(2)
 
+        for c in (0, 1, 4):
+            spread_bias(c)
+        nc.scalar.copy(out=sin_f[:], in_=sin_b[:])
+        for c in (2, 3, 5):
+            spread_bias(c)
+
         tables = []
 
         def make_tables():
-            for q, width in enumerate((8, 4)):
-                t = tab_pool.tile([P, width * HD], BF16, name="tab%d" % q)
-                for k in range(width // 4):
-                    t0 = 8 * q + 4 * k
-                    nc.tensor.matmul(
-                        out=t[:, 4 * HD * k : 4 * HD * (k + 1)],
-                        lhsT=ident[:],
-                        rhs=cos2[:, t0 : t0 + 4, :].rearrange("p t n -> p (t n)"),
-                        start=True,
-                        stop=True,
-                    )
-                tables.append(t)
+            t = tab_pool.tile([P, TILES * HALF], BF16, name="tab")
+            for t0, t1 in ((0, 8), (8, 12)):
+                nc.tensor.matmul(
+                    out=t[:, HALF * t0 : HALF * t1],
+                    lhsT=ident[:],
+                    rhs=cos_b[:, t0:t1, :].rearrange("p t n -> p (t n)"),
+                    start=True,
+                    stop=True,
+                )
+            tables.append(t)
 
         def window_of(tiles_of, splits, t, g, width):
             i = [k for k, (t0, t1) in enumerate(splits) if t0 <= t < t1][0]
@@ -170,12 +181,12 @@ def tile_multiheadattentionusingsdp_pa_kernel(
 
         def cosine_product(unit, part):
             t = unit["t"]
-            cos = tables[t // 8][:, HD * (t % 8) : HD * (t % 8) + HD]
+            cos = tables[0][:, HALF * t : HALF * (t + 1)]
             c0 = part * (UNIT // 2)
             nc.vector.tensor_tensor(
-                out=unit["m"][:, c0 : c0 + UNIT // 2].rearrange("p (h d) -> p h d", d=HD),
-                in0=unit["u"][:, c0 : c0 + UNIT // 2].rearrange("p (h d) -> p h d", d=HD),
-                in1=cos.unsqueeze(1).to_broadcast([P, HEADS // 2, HD]),
+                out=unit["m"][:, c0 : c0 + UNIT // 2].rearrange("p (g d) -> p g d", d=HALF),
+                in0=unit["u"][:, c0 : c0 + UNIT // 2].rearrange("p (g d) -> p g d", d=HALF),
+                in1=cos.unsqueeze(1).to_broadcast([P, HEADS, HALF]),
                 op=MULT,
             )
 

@@ -26,7 +26,7 @@ UNIT = HEADS * HD
 X_PLANE_SPLITS = ((0, 4), (4, 12))
 X_CODE_SPLITS = ((0, 2), (2, 4), (4, 12))
 V_HELD_BACK = 8
-STORE_LAG = 10
+STORE_LAG = 12
 VECTOR_COMBINES = 1
 VECTOR_COMBINE_LAG = 5
 
@@ -256,8 +256,8 @@ def tile_multiheadattentionusingsdp_pa_kernel(
                         "t": t,
                         "w_id": w,
                         "u": work.tile([P, UNIT], F32, name="u"),
-                        "m": work.tile([P, UNIT], F32, name="m"),
-                        "w": work.tile([P, HALF, 2 * HEADS], F32, name="w"),
+                        "m": work.tile([P, UNIT], F32, name="m", bufs=5),
+                        "w": work.tile([P, HALF, 2 * HEADS], F32, name="w", bufs=4),
                         "left": 4,
                     }
                 unit = units[(t, w)]

from contextlib import ExitStack

import concourse.mybir as mybir
from concourse.masks import make_identity

F32 = mybir.dt.float32
BF16 = mybir.dt.bfloat16
U8 = mybir.dt.uint8
I32 = mybir.dt.int32
FP4X4 = mybir.dt.float4_e2m1fn_x4
ADD = mybir.AluOpType.add
SUB = mybir.AluOpType.subtract
MULT = mybir.AluOpType.mult
COPY = mybir.ActivationFunctionType.Copy

S, D, HD = 1536, 2048, 128
HALF = HD // 2
HEADS = 16
FLOPS = 2 * S * D * 3 * D

P = 128
PASSES = D // 512
BLOCK = 512
TILES = S // P
UNIT = HEADS * HD
X_PLANE_SPLITS = ((0, 4), (4, 12))
X_CODE_SPLITS = ((0, 2), (2, 4), (4, 12))
V_HELD_BACK = 8
STORE_LAG = 12
VECTOR_COMBINES = 1
VECTOR_COMBINE_LAG = 5


def tile_multiheadattentionusingsdp_pa_kernel(
    tc, x_words, x_scales, w_qkv_words, w_qkv_scales, b_qkv, rope_cos, rope_sin, out_0, out_1, out_2
):
    nc = tc.nc
    outs = (out_0, out_1, out_2)
    with ExitStack() as ctx:
        keep = ctx.enter_context(tc.tile_pool(name="keep", bufs=1))
        work = ctx.enter_context(tc.tile_pool(name="work", bufs=3))
        acc_pool = ctx.enter_context(tc.psum_pool(name="acc", bufs=7))
        tab_pool = ctx.enter_context(tc.psum_pool(name="tab", bufs=1))
        ctx.enter_context(tc.manual_schedule())

        x_codes = [
            keep.tile([P, PASSES, 256 * (t1 - t0)], U8, name="x_codes%d" % i, align_bytes=64)
            for i, (t0, t1) in enumerate(X_CODE_SPLITS)
        ]
        x_planes = [
            keep.tile([P, PASSES, P * (t1 - t0)], U8, name="x_planes%d" % i, align_bytes=64)
            for i, (t0, t1) in enumerate(X_PLANE_SPLITS)
        ]
        w_planes = [keep.tile([P, PASSES, 2 * BLOCK], U8, name="w_planes%d" % c, align_bytes=64) for c in range(6)]
        w_codes = [keep.tile([P, PASSES, 2 * BLOCK], U8, name="w_codes%d" % j, align_bytes=64) for j in range(12)]
        bias = [keep.tile([P, 2 * BLOCK], BF16, name="bias%d" % c) for c in range(6)]
        cos_b = keep.tile([P, TILES, HALF], BF16, name="cos_b")
        b_rows = keep.tile([P, 3 * BLOCK], BF16, name="b_rows")
        sin_b = keep.tile([P, TILES, HALF], BF16, name="sin_b")
        sin_f = keep.tile([P, TILES, HALF], F32, name="sin_f")
        ident = keep.tile([P, P], BF16, name="ident")

        nc.vector.memset(b_rows[:], 0.0)
        nc.scalar.dma_start(out=b_rows[0:4, :], in_=b_qkv.rearrange("(k n) -> k n", k=4))
        nc.vector.memset(x_planes[0][:].bitcast(I32), 0)
        for c in (0, 1, 4):
            nc.vector.memset(w_planes[c][:].bitcast(I32), 0)
        nc.vector.memset(x_planes[1][:].bitcast(I32), 0)
        for c in (2, 3, 5):
            nc.vector.memset(w_planes[c][:].bitcast(I32), 0)

        make_identity(nc, ident[:])
        nc.gpsimd.dma_start(out=cos_b[:], in_=rope_cos.rearrange("(t p) d -> p t d", p=P))
        nc.gpsimd.dma_start(out=sin_b[:], in_=rope_sin.rearrange("(t p) d -> p t d", p=P))

        def load_planes(planes, scales, c0, c1):
            for q in range(4):
                nc.sync.dma_start(
                    out=planes[32 * q : 32 * q + 4, :, :].bitcast(I32),
                    in_=scales[:, 4 * q : 4 * q + 4, c0:c1].rearrange("g r n -> r g n").bitcast(I32),
                )

        def load_codes(codes, words, c0, c1):
            nc.sync.dma_start(
                out=codes[:].bitcast(I32),
                in_=words[:, :, 2 * c0 : 2 * c1].rearrange("g p n -> p g n").bitcast(I32),
            )

        def load_x_planes(i):
            t0, t1 = X_PLANE_SPLITS[i]
            load_planes(x_planes[i], x_scales, P * t0, P * t1)

        def load_x_codes(i):
            t0, t1 = X_CODE_SPLITS[i]
            load_codes(x_codes[i], x_words, P * t0, P * t1)

        def load_chunk_planes(c):
            load_planes(w_planes[c], w_qkv_scales, 2 * BLOCK * c, 2 * BLOCK * (c + 1))

        def spread_bias(c):
            spread = acc_pool.tile([P, 2 * BLOCK], BF16, name="acc")
            for half in range(2):
                n = 2 * c + half
                nc.tensor.matmul(
                    out=spread[:, BLOCK * half : BLOCK * (half + 1)],
                    lhsT=ident[:, n // 3 : n // 3 + 1].to_broadcast([P, P]),
                    rhs=b_rows[:, BLOCK * (n % 3) : BLOCK * (n % 3 + 1)],
                    start=True,
                    stop=True,
                )
            nc.scalar.copy(out=bias[c][:], in_=spread[:])

        def load_block(j):
            load_codes(w_codes[j], w_qkv_words, BLOCK * j, BLOCK * (j + 1))

        def load_chunk(c):
            load_chunk_planes(c)
            load_block(2 * c)
            load_block(2 * c + 1)

        load_x_codes(0)
        load_block(0)
        load_x_planes(0)
        load_chunk_planes(0)
        load_block(1)
        load_chunk(1)
        load_x_codes(1)
        load_chunk(4)
        load_x_planes(1)
        load_x_codes(2)

        for c in (0, 1, 4):
            spread_bias(c)
        nc.scalar.copy(out=sin_f[:], in_=sin_b[:])
        for c in (2, 3, 5):
            spread_bias(c)

        tables = []

        def make_tables():
            t = tab_pool.tile([P, TILES * HALF], BF16, name="tab")
            for t0, t1 in ((0, 8), (8, 12)):
                nc.tensor.matmul(
                    out=t[:, HALF * t0 : HALF * t1],
                    lhsT=ident[:],
                    rhs=cos_b[:, t0:t1, :].rearrange("p t n -> p (t n)"),
                    start=True,
                    stop=True,
                )
            tables.append(t)

        def window_of(tiles_of, splits, t, g, width):
            i = [k for k, (t0, t1) in enumerate(splits) if t0 <= t < t1][0]
            c0 = width * (t - splits[i][0])
            return tiles_of[i][:, g, c0 : c0 + width]

        def project(t, j):
            acc = acc_pool.tile([P, BLOCK], F32, name="acc")
            o = BLOCK * (j % 2)
            for g in range(PASSES):
                nc.tensor.matmul_mx(
                    out=acc[:],
                    lhsT=window_of(x_codes, X_CODE_SPLITS, t, g, 256).bitcast(FP4X4),
                    lhsT_scale=window_of(x_planes, X_PLANE_SPLITS, t, g, P),
                    rhs=w_codes[j][:, g, :].bitcast(FP4X4),
                    rhs_scale=w_planes[j // 2][:, g, o : o + BLOCK],
                    start=(g == 0),
                    stop=(g == PASSES - 1),
                )
            return acc

        def add_bias(dst, acc, j):
            o = BLOCK * (j % 2)
            nc.vector.tensor_tensor(out=dst, in0=acc[:], in1=bias[j // 2][:, o : o + BLOCK], op=ADD)

        def store(which, h0, nh, t, src):
            nc.sync.dma_start(
                out=outs[which][0, h0 : h0 + nh, P * t : P * (t + 1), :].rearrange("h s d -> s h d"),
                in_=src.rearrange("p (h d) -> p h d", d=HD),
            )

        def cosine_product(unit, part):
            t = unit["t"]
            cos = tables[0][:, HALF * t : HALF * (t + 1)]
            c0 = part * (UNIT // 2)
            nc.vector.tensor_tensor(
                out=unit["m"][:, c0 : c0 + UNIT // 2].rearrange("p (g d) -> p g d", d=HALF),
                in0=unit["u"][:, c0 : c0 + UNIT // 2].rearrange("p (g d) -> p g d", d=HALF),
                in1=cos.unsqueeze(1).to_broadcast([P, HEADS, HALF]),
                op=MULT,
            )

        def sine_products(unit):
            t = unit["t"]
            u4 = unit["u"][:].rearrange("p (h f d) -> p h f d", f=2, d=HALF)
            for d in range(HALF):
                nc.scalar.activation(
                    out=unit["w"][:, d, :].rearrange("p (h f) -> p h f", f=2),
                    in_=u4[:, :, :, d],
                    func=COPY,
                    scale=sin_f[:, t, d : d + 1],
                )

        def combine(unit, engine, half):
            m3 = unit["m"][:].rearrange("p (h d) -> p h d", d=HD)
            wv = unit["w"][:].rearrange("p d (h f) -> p f h d", f=2)
            c0 = HALF * half
            engine.tensor_tensor(
                out=m3[:, :, c0 : c0 + HALF], in0=m3[:, :, c0 : c0 + HALF], in1=wv[:, 1 - half], op=(ADD if half else SUB)
            )

        def store_unit(unit):
            store(unit["w_id"], 0, HEADS, unit["t"], unit["m"][:])

        rope_units = [(t, w) for w in range(2) for t in range(TILES)]
        value_jobs = [(t, 8 + 2 * w + k) for w in range(2) for t in range(TILES) for k in range(2)]
        woven = len(value_jobs) - V_HELD_BACK
        jobs = [(t, j) for j in range(4) for t in (0, 1)]
        drawn = 0
        for i, (t, w) in enumerate(rope_units):
            if i >= 2:
                jobs += [(t, 4 * w + k) for k in range(4)]
            if i >= 1:
                quota = (woven * (i + 1)) // len(rope_units)
                jobs += value_jobs[drawn:quota]
                drawn = quota
        jobs += value_jobs[drawn:]

        late_loads = {14: 2, 26: 3, 38: 5}
        units = {}
        values = {}
        pending = []
        deferred = []
        n_done = 0

        def run_deferred(now):
            ready = sorted([e for e in deferred if e[0] <= now], key=lambda e: e[0])
            for e in ready:
                deferred.remove(e)
                e[1]()

        def vector_tail(unit, half):
            combine(unit, nc.vector, half)
            if half == 1:
                store_unit(unit)

        for step, (t, j) in enumerate(jobs):
            acc = project(t, j)
            if step == 3:
                make_tables()
            done = False
            if j < 8:
                w = j // 4
                if (t, w) not in units:
                    units[(t, w)] = {
                        "t": t,
                        "w_id": w,
                        "u": work.tile([P, UNIT], F32, name="u"),
                        "m": work.tile([P, UNIT], F32, name="m", bufs=5),
                        "w": work.tile([P, HALF, 2 * HEADS], F32, name="w", bufs=4),
                        "left": 4,
                    }
                unit = units[(t, w)]
                o = BLOCK * (j % 4)
                add_bias(unit["u"][:, o : o + BLOCK], acc, j)
                unit["left"] -= 1
                done = unit["left"] == 0
            else:
                w = (j - 8) // 2
                if (t, w) not in values:
                    values[(t, w)] = work.tile([P, 2 * BLOCK], F32, name="v", bufs=5)
                v = values[(t, w)]
                o = BLOCK * (j % 2)
                add_bias(v[:, o : o + BLOCK], acc, j)
                if step >= len(jobs) - 2:
                    store(2, 4 * (j - 8), 4, t, v[:, o : o + BLOCK])
                elif j % 2 == 1:
                    store(2, 8 * w, 8, t, v[:])
            if pending:
                pu, part = pending.pop(0)
                cosine_product(pu, part)
                if part == 1 and not pu["on_vector"]:
                    combine(pu, nc.gpsimd, 0)
                    combine(pu, nc.gpsimd, 1)
                    deferred.append((step + STORE_LAG, lambda u=pu: store_unit(u)))
            run_deferred(step)
            if done:
                n_done += 1
                unit["on_vector"] = n_done > len(rope_units) - VECTOR_COMBINES
                sine_products(unit)
                pending.append((unit, 0))
                pending.append((unit, 1))
                if unit["on_vector"]:
                    deferred.append((step + VECTOR_COMBINE_LAG, lambda u=unit: vector_tail(u, 0)))
                    deferred.append((step + VECTOR_COMBINE_LAG + 1, lambda u=unit: vector_tail(u, 1)))
            if step in late_loads:
                load_chunk(late_loads[step])
        run_deferred(len(jobs) + 100)
